import numpy as np
import ml_dtypes


def mxq(x, axis, fmt="e4m3"):
    dtype, down = {"e4m3": (ml_dtypes.float8_e4m3fn, 7), "e5m2": (ml_dtypes.float8_e5m2, 14)}[fmt]
    v = np.moveaxis(np.asarray(x, np.float32).astype(ml_dtypes.bfloat16).astype(np.float64), axis, -1)
    blocks = v.reshape(v.shape[:-1] + (-1, 32))
    amax = np.abs(blocks).max(-1, keepdims=True)
    byte = np.maximum(np.where(amax > 0, np.frexp(amax)[1] - 1 + 127, 0) - down, 1)
    scale = np.exp2(byte - 127.0)
    codes = (blocks / scale).astype(np.float32).astype(dtype).astype(np.float64)
    return np.moveaxis((codes * scale).reshape(v.shape), -1, axis)


WIDE = False


def mx_kscale(k):
    if not WIDE:
        return np.ones(k)
    levels = np.array([10, -10, 5, -5, 0])
    a = np.random.permutation(np.resize(levels, k // 512 * 4)).reshape(k // 512, 4)
    idx = np.arange(k)
    return np.exp2(a[idx // 512, idx % 128 // 32])


BF16 = ml_dtypes.bfloat16


def bf(x):
    return np.asarray(x, np.float32).astype(BF16)


def f64(x):
    return np.asarray(x).astype(np.float64)


B, H, W, NP, C, CO = 16, 8, 9, 9, 512, 512
SHIFTS = ((0, 0), (0, 0), (0, 0), (0, -1), (0, 1), (1, -1), (1, 1), (-1, -1), (-1, 1))


def setup_inputs():
    s = mx_kscale(C)
    t = mx_kscale(NP * CO)
    return {
        "xa": bf(np.random.standard_normal((B, C, H, W)) * 0.65 * s[None, :, None, None]),
        "W9": bf(np.random.standard_normal((NP, CO, C)) / np.sqrt(C) * t.reshape(NP, CO, 1) / s[None, None, :]),
        "b9": bf(np.random.standard_normal((NP, CO)) * 0.3 * t.reshape(NP, CO)),
        "Wf": bf(np.random.standard_normal((C, NP * CO)) / np.sqrt(NP * CO) / t[None, :]),
        "b_fuse": bf(np.random.standard_normal(C) * 0.3),
    }


def reference(xa, W9, b9, Wf, b_fuse):
    y = mxq(f64(W9).reshape(NP * CO, C), 1, "e4m3") @ mxq(f64(xa).reshape(B, C, H * W), 1, "e4m3")
    y = (y + f64(b9).reshape(NP * CO)[None, :, None]).reshape(B, NP, CO, H, W)
    out = np.zeros((B, C, H, W)) + f64(b_fuse)[None, :, None, None]
    for k, (dh, dw) in enumerate(SHIFTS):
        hn, wn = H - abs(dh), W - abs(dw)
        hs, ws = max(dh, 0), max(dw, 0)
        hd, wd = max(-dh, 0), max(-dw, 0)
        src = y[:, k, :, hs:hs + hn, ws:ws + wn].reshape(B, CO, hn * wn)
        p = mxq(f64(Wf)[:, k * CO:(k + 1) * CO], 1, "e4m3") @ mxq(src, 1, "e4m3")
        out[:, :, hd:hd + hn, wd:wd + wn] += p.reshape(B, C, hn, wn)
    return out

@@ -1,0 +1,344 @@
+from contextlib import ExitStack
+
+import concourse.mybir as mybir
+from concourse.masks import make_identity
+
+F32 = mybir.dt.float32
+BF16 = mybir.dt.bfloat16
+U32 = mybir.dt.uint32
+U8 = mybir.dt.uint8
+FP8X4 = mybir.dt.float8_e4m3fn_x4
+IDENTITY = mybir.ActivationFunctionType.Identity
+ADD = mybir.AluOpType.add
+
+B, C, H, W, NP, CO = 16, 512, 8, 9, 9, 512
+SHIFTS = ((0, 0), (0, 0), (0, 0), (0, -1), (0, 1), (1, -1), (1, 1), (-1, -1), (-1, 1))
+USED = sum((H - abs(dh)) * (W - abs(dw)) for dh, dw in SHIFTS)
+FLOPS = 2 * NP * CO * C * B * H * W + 2 * C * CO * B * USED
+
+P = 128
+PACK = 4
+PAIR = 2
+HALVES = 2
+HALF_B = B // HALVES
+STRIP = H * HALF_B
+MAIN_COLS = (W - 1) * STRIP
+EDGE_COLS = H * B
+X_HALF = W * STRIP
+X_MAIN = 2 * EDGE_COLS
+X_COLS = X_MAIN + HALVES * X_HALF
+RUN = 4
+
+PREP_AHEAD = 2
+PACK_LAG = 1
+FUSE_LAG = 2
+
+
+def column_tiles():
+    main = [
+        dict(
+            name="main%d" % g,
+            strips=W - 1,
+            strip_cols=STRIP,
+            row=HALF_B,
+            x_base=X_MAIN + g * X_HALF,
+            x_step=STRIP,
+            pillars=list(range(NP)),
+            half=g,
+        )
+        for g in range(HALVES)
+    ]
+    edge = dict(
+        name="edge",
+        strips=1,
+        strip_cols=EDGE_COLS,
+        row=B,
+        x_base=EDGE_COLS,
+        x_step=EDGE_COLS,
+        pillars=[k for k in range(NP) if SHIFTS[k][1] <= 0],
+        half=None,
+    )
+    return [main[0], edge, main[1]]
+
+
+def valid_part(ct, k):
+    dh, dw = SHIFTS[k]
+    first_strip = 1 if (ct["half"] is not None and dw < 0) else 0
+    return first_strip, max(-dh, 0), H - abs(dh)
+
+
+def tile_shiftedpillarsconcatentation_bnact_np9_pa_kernel(tc, xa, W9, b9, Wf, b_fuse, out):
+    nc = tc.nc
+    tiles = column_tiles()
+    items = [(ct, k) for ct in tiles for k in ct["pillars"]]
+
+    with ExitStack() as stack:
+        keep = stack.enter_context(tc.tile_pool(name="keep", bufs=1))
+        raw_pool = stack.enter_context(tc.tile_pool(name="raw", bufs=4))
+        flow = stack.enter_context(tc.tile_pool(name="flow", bufs=3))
+        work = stack.enter_context(tc.psum_pool(name="work", bufs=4))
+        accs = stack.enter_context(tc.psum_pool(name="accs", bufs=PACK))
+
+        x_raw = []
+        w9_raw = []
+        wf_raw = []
+
+        def load_x(g):
+            xr = keep.tile([P, HALF_B, PACK, H * W], BF16, name="x_raw%d" % g)
+            nc.sync.dma_start(
+                out=xr[:].rearrange("p b (u e) s -> p (b u) (e s)", u=PAIR),
+                in_=xa[g * HALF_B : (g + 1) * HALF_B].rearrange(
+                    "b (u p e) h w -> p (b u) (e h w)", u=PAIR, e=PAIR
+                ),
+            )
+            x_raw.append(xr)
+
+        def load_weights(k):
+            w9r = raw_pool.tile([P, PACK, C], BF16, tag="w9_raw", name="w9_raw%d" % k)
+            nc.sync.dma_start(
+                out=w9r[:].rearrange("p (u e) c -> p u (e c)", u=PAIR),
+                in_=W9[k].rearrange("(u p e) c -> p u (e c)", u=PAIR, e=PAIR),
+            )
+            w9_raw.append(w9r)
+            wfr = raw_pool.tile([P, PACK, CO], BF16, tag="wf_raw", name="wf_raw%d" % k)
+            for u in range(PAIR):
+                nc.sync.dma_start(
+                    out=wfr[:, PAIR * u : PAIR * (u + 1), :],
+                    in_=Wf[u * PAIR * P : (u + 1) * PAIR * P, k * CO : (k + 1) * CO].rearrange(
+                        "(p e) j -> p e j", e=PAIR
+                    ),
+                )
+            wf_raw.append(wfr)
+
+        load_x(0)
+        load_weights(0)
+        load_weights(1)
+        load_x(1)
+        for k in range(2, NP):
+            load_weights(k)
+
+        ident = keep.tile([P, P], F32, name="ident")
+        make_identity(nc, ident[:])
+
+        bias_rows = keep.tile([P, PAIR * P], BF16, name="bias_rows")
+        nc.vector.memset(bias_rows[:], 0.0)
+        n_b9 = NP * PAIR
+        n_rows = n_b9 + PAIR
+        nc.scalar.dma_start(out=bias_rows[0:n_b9, :], in_=b9.rearrange("k (u c) -> (k u) c", u=PAIR))
+        nc.scalar.dma_start(out=bias_rows[n_b9:n_rows, :], in_=b_fuse.rearrange("(u c) -> u c", u=PAIR))
+        bias_ps = work.tile([P, P], F32, tag="work", name="bias_ps")
+        nc.tensor.transpose(bias_ps[:], bias_rows[:].bitcast(F32), ident[:])
+        bias_pairs = keep.tile([P, n_rows], F32, name="bias_pairs")
+        nc.vector.tensor_copy(out=bias_pairs[:], in_=bias_ps[:, 0:n_rows])
+        bias = keep.tile([P, PAIR * n_rows], F32, name="bias")
+        nc.vector.tensor_copy(out=bias[:], in_=bias_pairs[:].bitcast(BF16))
+        fuse_bias = NP * PACK
+
+        stage = {}
+        for ct in tiles:
+            kind = ct["strip_cols"]
+            for k in ct["pillars"]:
+                if (kind, k) in stage:
+                    continue
+                st = keep.tile(
+                    [P, ct["strips"] * ct["strip_cols"], PACK], BF16, name="stage%d_%d" % (kind, k), align_bytes=64
+                )
+                stage[(kind, k)] = st
+                first_strip, first_row, rows = valid_part(ct, k)
+                view = st[:].rearrange("p (w s) t -> p w s t", w=ct["strips"])
+                if first_strip:
+                    nc.vector.memset(view[:, 0:first_strip], 0.0)
+                if rows < H:
+                    empty_row = 0 if first_row else H - 1
+                    nc.vector.memset(view[:, :, empty_row * ct["row"] : (empty_row + 1) * ct["row"], :], 0.0)
+
+        x_grouped = keep.tile([P, X_COLS, PACK], BF16, name="x_grouped", align_bytes=64)
+        x_codes = keep.tile([P, X_COLS], U32, name="x_codes", align_bytes=64)
+        x_scales = keep.tile([P, X_COLS], U8, name="x_scales", align_bytes=64)
+
+        def regroup_x_main(g):
+            lo = X_MAIN + g * X_HALF
+            nc.vector.tensor_copy(
+                out=x_grouped[:, lo : lo + X_HALF, :].rearrange("p (w h b) t -> p w h b t", w=W, h=H),
+                in_=x_raw[g][:].rearrange("p b t (h w) -> p w h b t", w=W),
+            )
+
+        def regroup_x_edge(g):
+            nc.vector.tensor_copy(
+                out=x_grouped[:, 0:X_MAIN, :].rearrange("p (w h g b) t -> p w h g b t", w=2, h=H, g=HALVES)[
+                    :, :, :, g, :, :
+                ],
+                in_=x_raw[g][:].rearrange("p b t (h w) -> p w h b t", w=W)[:, W - 2 : W],
+            )
+
+        def quantise_x(lo, cols):
+            nc.vector.quantize_mx(
+                out=x_codes[:, lo : lo + cols].bitcast(FP8X4),
+                scales=x_scales[:, lo : lo + cols],
+                in_=x_grouped[:, lo : lo + cols, :].rearrange("p c t -> p (c t)"),
+            )
+
+        regroup_x_main(0)
+        regroup_x_edge(0)
+        quantise_x(X_MAIN, 512)
+        regroup_x_edge(1)
+        regroup_x_main(1)
+        quantise_x(0, X_MAIN)
+        quantise_x(X_MAIN + 512, 512)
+        quantise_x(X_MAIN + 1024, 128)
+
+        w9_codes = keep.tile([P, NP, CO], U32, name="w9_codes", align_bytes=64)
+        w9_scales = keep.tile([P, NP, CO], U8, name="w9_scales", align_bytes=64)
+        wf_codes = keep.tile([P, NP, C], U32, name="wf_codes", align_bytes=64)
+        wf_scales = keep.tile([P, NP, C], U8, name="wf_scales", align_bytes=64)
+        banks_emptied = [0]
+
+        def transpose_and_quantise(raw, codes, scales):
+            words = raw[:].bitcast(F32)
+            grouped = flow.tile([P, PACK * P * PACK], BF16, tag="w_grouped", name="w_grouped", bufs=4, align_bytes=64)
+            grouped_words = grouped[:].bitcast(F32)
+            for pair_of_tiles in range(PACK // 2):
+                bank = work.tile([P, PAIR, 2 * P], F32, tag="work", name="w_bank")
+                for i in range(2):
+                    for u in range(PAIR):
+                        nc.tensor.transpose(
+                            bank[:, u, i * P : (i + 1) * P],
+                            words[:, 2 * pair_of_tiles + i, u * P : (u + 1) * P],
+                            ident[:],
+                        )
+                dst = grouped_words[:, pair_of_tiles * 4 * P : (pair_of_tiles + 1) * 4 * P].rearrange(
+                    "p (c u) -> p c u", u=PAIR
+                )
+                src = bank[:].rearrange("p u c -> p c u")
+                if banks_emptied[0] % 4 == 3:
+                    nc.vector.tensor_copy(out=dst, in_=src)
+                else:
+                    nc.scalar.copy(out=dst, in_=src)
+                banks_emptied[0] += 1
+            nc.vector.quantize_mx(out=codes.bitcast(FP8X4), scales=scales, in_=grouped[:])
+
+        def prepare_weights(k):
+            transpose_and_quantise(w9_raw[k], w9_codes[:, k, :], w9_scales[:, k, :])
+            transpose_and_quantise(wf_raw[k], wf_codes[:, k, :], wf_scales[:, k, :])
+
+        planes_of = {}
+        cat_of = {}
+        acc_of = {}
+        out_sb = [keep.tile([P, B, PAIR, H * W], F32, name="out_sb%d" % u) for u in range(PAIR)]
+        finished = set()
+
+        def project(n):
+            ct, k = items[n]
+            dh, dw = SHIFTS[k]
+            cols = ct["strips"] * ct["strip_cols"]
+            x_lo = ct["x_base"] + dw * ct["x_step"]
+            first_strip, first_row, rows = valid_part(ct, k)
+            dst_lo = first_row * ct["row"]
+            src_lo = (first_row + dh) * ct["row"]
+            span = rows * ct["row"]
+            planes = flow.tile([P, PACK, cols], BF16, tag="planes", name="planes")
+            planes_of[n] = planes
+            for t in range(PACK):
+                y_ps = work.tile([P, cols], F32, tag="work", name="y_ps")
+                nc.tensor.matmul_mx(
+                    out=y_ps[:],
+                    lhsT=w9_codes[:, k, t * P : (t + 1) * P].bitcast(FP8X4),
+                    lhsT_scale=w9_scales[:, k, t * P : (t + 1) * P],
+                    rhs=x_codes[:, x_lo : x_lo + cols].bitcast(FP8X4),
+                    rhs_scale=x_scales[:, x_lo : x_lo + cols],
+                    start=True,
+                    stop=True,
+                )
+                nc.scalar.activation(
+                    out=planes[:, t, :].rearrange("p (w s) -> p w s", w=ct["strips"])[
+                        :, first_strip:, dst_lo : dst_lo + span
+                    ],
+                    in_=y_ps[:].rearrange("p (w s) -> p w s", w=ct["strips"])[:, first_strip:, src_lo : src_lo + span],
+                    func=IDENTITY,
+                    bias=bias[:, k * PACK + t : k * PACK + t + 1],
+                    scale=1.0,
+                )
+
+        def pack(n):
+            ct, k = items[n]
+            cols = ct["strips"] * ct["strip_cols"]
+            first_strip, first_row, rows = valid_part(ct, k)
+            lo = first_row * ct["row"] // RUN
+            hi = lo + rows * ct["row"] // RUN
+            st = stage[(ct["strip_cols"], k)]
+            nc.vector.tensor_copy(
+                out=st[:].rearrange("p (w c i) t -> p w c t i", w=ct["strips"], i=RUN)[:, first_strip:, lo:hi],
+                in_=planes_of[n][:].rearrange("p t (w c i) -> p w c t i", w=ct["strips"], i=RUN)[
+                    :, first_strip:, lo:hi
+                ],
+            )
+            codes = flow.tile([P, cols], U32, tag="cat_codes", name="cat_codes", align_bytes=64)
+            scales = flow.tile([P, cols], U8, tag="cat_scales", name="cat_scales", align_bytes=64)
+            nc.vector.quantize_mx(
+                out=codes[:].bitcast(FP8X4), scales=scales[:], in_=st[:].rearrange("p c t -> p (c t)")
+            )
+            cat_of[n] = (codes, scales)
+
+        def fuse(n):
+            ct, k = items[n]
+            cols = ct["strips"] * ct["strip_cols"]
+            codes, scales = cat_of[n]
+            first = k == ct["pillars"][0]
+            last = k == ct["pillars"][-1]
+            for t in range(PACK):
+                if first:
+                    acc_of[t] = accs.tile([P, cols], F32, tag="acc", name="acc")
+                nc.tensor.matmul_mx(
+                    out=acc_of[t][:],
+                    lhsT=wf_codes[:, k, t * P : (t + 1) * P].bitcast(FP8X4),
+                    lhsT_scale=wf_scales[:, k, t * P : (t + 1) * P],
+                    rhs=codes[:].bitcast(FP8X4),
+                    rhs_scale=scales[:],
+                    start=first,
+                    stop=last,
+                )
+            if last:
+                for t in range(PACK):
+                    empty_accumulator(ct, t)
+                finished.add(ct["name"])
+                for g in range(HALVES):
+                    if ("main%d" % g) in finished and "edge" in finished and ("stored%d" % g) not in finished:
+                        finished.add("stored%d" % g)
+                        store(g)
+
+        def empty_accumulator(ct, t):
+            u, e = divmod(t, PAIR)
+            image = out_sb[u][:, :, e, :].rearrange("p b (h w) -> p b h w", w=W)
+            if ct["half"] is None:
+                dst = image[:, :, :, W - 1]
+                src = acc_of[t][:].rearrange("p (h b) -> p b h", h=H)
+            else:
+                g = ct["half"]
+                dst = image[:, g * HALF_B : (g + 1) * HALF_B, :, 0 : W - 1]
+                src = acc_of[t][:].rearrange("p (w h b) -> p b h w", w=W - 1, h=H)
+            b_col = bias[:, fuse_bias + t : fuse_bias + t + 1]
+            if e == 0:
+                nc.vector.tensor_scalar(out=dst, in0=src, scalar1=b_col, scalar2=None, op0=ADD)
+            else:
+                nc.scalar.activation(out=dst, in_=src, func=IDENTITY, bias=b_col, scale=1.0)
+
+        def store(g):
+            for u in range(PAIR):
+                nc.sync.dma_start(
+                    out=out[g * HALF_B : (g + 1) * HALF_B, u * PAIR * P : (u + 1) * PAIR * P].rearrange(
+                        "b (p e) h w -> p b (e h w)", e=PAIR
+                    ),
+                    in_=out_sb[u][:, g * HALF_B : (g + 1) * HALF_B].rearrange("p b e s -> p b (e s)"),
+                )
+
+        for k in range(PREP_AHEAD):
+            prepare_weights(k)
+        for step in range(len(items) + FUSE_LAG):
+            if step + PREP_AHEAD < NP:
+                prepare_weights(step + PREP_AHEAD)
+            if step < len(items):
+                project(step)
+            if 0 <= step - PACK_LAG < len(items):
+                pack(step - PACK_LAG)
+            if 0 <= step - FUSE_LAG:
+                fuse(step - FUSE_LAG)

@@ -5,6 +5,7 @@ from concourse.masks import make_identity
 
 F32 = mybir.dt.float32
 BF16 = mybir.dt.bfloat16
+I32 = mybir.dt.int32
 U32 = mybir.dt.uint32
 U8 = mybir.dt.uint8
 FP8X4 = mybir.dt.float8_e4m3fn_x4
@@ -25,11 +26,13 @@ STRIP = H * HALF_B
 MAIN_COLS = (W - 1) * STRIP
 EDGE_COLS = H * B
 X_HALF = W * STRIP
-X_MAIN = 2 * EDGE_COLS
-X_COLS = X_MAIN + HALVES * X_HALF
+X_PAD = STRIP
+X_EDGE = X_PAD + HALVES * X_HALF
+X_COLS = X_EDGE + 2 * EDGE_COLS
 RUN = 4
 
-PREP_AHEAD = 2
+RAW_BUFS = 4
+AHEAD = 2
 PACK_LAG = 1
 FUSE_LAG = 2
 
@@ -38,25 +41,25 @@ def column_tiles():
     main = [
         dict(
             name="main%d" % g,
+            half=g,
             strips=W - 1,
             strip_cols=STRIP,
             row=HALF_B,
-            x_base=X_MAIN + g * X_HALF,
+            x_base=X_PAD + g * X_HALF,
             x_step=STRIP,
             pillars=list(range(NP)),
-            half=g,
         )
         for g in range(HALVES)
     ]
     edge = dict(
         name="edge",
+        half=None,
         strips=1,
         strip_cols=EDGE_COLS,
         row=B,
-        x_base=EDGE_COLS,
+        x_base=X_EDGE + EDGE_COLS,
         x_step=EDGE_COLS,
         pillars=[k for k in range(NP) if SHIFTS[k][1] <= 0],
-        half=None,
     )
     return [main[0], edge, main[1]]
 
@@ -73,49 +76,51 @@ def tile_shiftedpillarsconcatentation_bnact_np9_pa_kernel(tc, xa, W9, b9, Wf, b_
     items = [(ct, k) for ct in tiles for k in ct["pillars"]]
 
     with ExitStack() as stack:
+        stack.enter_context(tc.manual_schedule())
         keep = stack.enter_context(tc.tile_pool(name="keep", bufs=1))
-        raw_pool = stack.enter_context(tc.tile_pool(name="raw", bufs=4))
+        raw_pool = stack.enter_context(tc.tile_pool(name="raw", bufs=RAW_BUFS))
         flow = stack.enter_context(tc.tile_pool(name="flow", bufs=3))
         work = stack.enter_context(tc.psum_pool(name="work", bufs=4))
         accs = stack.enter_context(tc.psum_pool(name="accs", bufs=PACK))
 
-        x_raw = []
-        w9_raw = []
-        wf_raw = []
+        x_raw = {}
+        w9_raw = {}
+        wf_raw = {}
 
         def load_x(g):
-            xr = keep.tile([P, HALF_B, PACK, H * W], BF16, name="x_raw%d" % g)
+            x_raw[g] = keep.tile([P, HALF_B, PACK, H * W], BF16, name="x_raw%d" % g)
             nc.sync.dma_start(
-                out=xr[:].rearrange("p b (u e) s -> p (b u) (e s)", u=PAIR),
+                out=x_raw[g][:].rearrange("p b (u e) s -> p (b u) (e s)", u=PAIR),
                 in_=xa[g * HALF_B : (g + 1) * HALF_B].rearrange(
                     "b (u p e) h w -> p (b u) (e h w)", u=PAIR, e=PAIR
                 ),
             )
-            x_raw.append(xr)
 
-        def load_weights(k):
-            w9r = raw_pool.tile([P, PACK, C], BF16, tag="w9_raw", name="w9_raw%d" % k)
+        def load_w9(k):
+            w9_raw[k] = raw_pool.tile([P, PACK, C], BF16, tag="w9_raw", name="w9_raw%d" % k)
             nc.sync.dma_start(
-                out=w9r[:].rearrange("p (u e) c -> p u (e c)", u=PAIR),
+                out=w9_raw[k][:].rearrange("p (u e) c -> p u (e c)", u=PAIR),
                 in_=W9[k].rearrange("(u p e) c -> p u (e c)", u=PAIR, e=PAIR),
             )
-            w9_raw.append(w9r)
-            wfr = raw_pool.tile([P, PACK, CO], BF16, tag="wf_raw", name="wf_raw%d" % k)
+
+        def load_wf(k):
+            wf_raw[k] = raw_pool.tile([P, PACK, CO], BF16, tag="wf_raw", name="wf_raw%d" % k)
             for u in range(PAIR):
                 nc.sync.dma_start(
-                    out=wfr[:, PAIR * u : PAIR * (u + 1), :],
+                    out=wf_raw[k][:, PAIR * u : PAIR * (u + 1), :],
                     in_=Wf[u * PAIR * P : (u + 1) * PAIR * P, k * CO : (k + 1) * CO].rearrange(
                         "(p e) j -> p e j", e=PAIR
                     ),
                 )
-            wf_raw.append(wfr)
 
+        load_w9(0)
         load_x(0)
-        load_weights(0)
-        load_weights(1)
-        load_x(1)
-        for k in range(2, NP):
-            load_weights(k)
+        load_wf(0)
+        for k in range(1, NP):
+            load_w9(k)
+            load_wf(k)
+            if k == RAW_BUFS - 1:
+                load_x(1)
 
         ident = keep.tile([P, P], F32, name="ident")
         make_identity(nc, ident[:])
@@ -128,24 +133,18 @@ def tile_shiftedpillarsconcatentation_bnact_np9_pa_kernel(tc, xa, W9, b9, Wf, b_
         nc.scalar.dma_start(out=bias_rows[n_b9:n_rows, :], in_=b_fuse.rearrange("(u c) -> u c", u=PAIR))
         bias_ps = work.tile([P, P], F32, tag="work", name="bias_ps")
         nc.tensor.transpose(bias_ps[:], bias_rows[:].bitcast(F32), ident[:])
-        bias_pairs = keep.tile([P, n_rows], F32, name="bias_pairs")
-        nc.vector.tensor_copy(out=bias_pairs[:], in_=bias_ps[:, 0:n_rows])
-        bias = keep.tile([P, PAIR * n_rows], F32, name="bias")
-        nc.vector.tensor_copy(out=bias[:], in_=bias_pairs[:].bitcast(BF16))
-        fuse_bias = NP * PACK
 
         stage = {}
         for ct in tiles:
-            kind = ct["strip_cols"]
             for k in ct["pillars"]:
-                if (kind, k) in stage:
+                key = (ct["strip_cols"], k)
+                if key in stage:
                     continue
-                st = keep.tile(
-                    [P, ct["strips"] * ct["strip_cols"], PACK], BF16, name="stage%d_%d" % (kind, k), align_bytes=64
+                stage[key] = keep.tile(
+                    [P, ct["strips"] * ct["strip_cols"], PACK], BF16, name="stage%d_%d" % key, align_bytes=64
                 )
-                stage[(kind, k)] = st
                 first_strip, first_row, rows = valid_part(ct, k)
-                view = st[:].rearrange("p (w s) t -> p w s t", w=ct["strips"])
+                view = stage[key][:].rearrange("p (w s) t -> p w s t", w=ct["strips"])
                 if first_strip:
                     nc.vector.memset(view[:, 0:first_strip], 0.0)
                 if rows < H:
@@ -155,21 +154,8 @@ def tile_shiftedpillarsconcatentation_bnact_np9_pa_kernel(tc, xa, W9, b9, Wf, b_
         x_grouped = keep.tile([P, X_COLS, PACK], BF16, name="x_grouped", align_bytes=64)
         x_codes = keep.tile([P, X_COLS], U32, name="x_codes", align_bytes=64)
         x_scales = keep.tile([P, X_COLS], U8, name="x_scales", align_bytes=64)
-
-        def regroup_x_main(g):
-            lo = X_MAIN + g * X_HALF
-            nc.vector.tensor_copy(
-                out=x_grouped[:, lo : lo + X_HALF, :].rearrange("p (w h b) t -> p w h b t", w=W, h=H),
-                in_=x_raw[g][:].rearrange("p b t (h w) -> p w h b t", w=W),
-            )
-
-        def regroup_x_edge(g):
-            nc.vector.tensor_copy(
-                out=x_grouped[:, 0:X_MAIN, :].rearrange("p (w h g b) t -> p w h g b t", w=2, h=H, g=HALVES)[
-                    :, :, :, g, :, :
-                ],
-                in_=x_raw[g][:].rearrange("p b t (h w) -> p w h b t", w=W)[:, W - 2 : W],
-            )
+        nc.vector.memset(x_codes[:, 0:X_PAD].bitcast(I32), 0)
+        nc.vector.memset(x_scales[:, 0:X_PAD].bitcast(I32), 0)
 
         def quantise_x(lo, cols):
             nc.vector.quantize_mx(
@@ -178,48 +164,48 @@ def tile_shiftedpillarsconcatentation_bnact_np9_pa_kernel(tc, xa, W9, b9, Wf, b_
                 in_=x_grouped[:, lo : lo + cols, :].rearrange("p c t -> p (c t)"),
             )
 
-        regroup_x_main(0)
-        regroup_x_edge(0)
-        quantise_x(X_MAIN, 512)
-        regroup_x_edge(1)
-        regroup_x_main(1)
-        quantise_x(0, X_MAIN)
-        quantise_x(X_MAIN + 512, 512)
-        quantise_x(X_MAIN + 1024, 128)
+        def prepare_x(ct):
+            if ct["half"] is None:
+                for g in range(HALVES):
+                    nc.vector.tensor_copy(
+                        out=x_grouped[:, X_EDGE:X_COLS, :].rearrange(
+                            "p (w h g b) t -> p w h g b t", w=2, h=H, g=HALVES
+                        )[:, :, :, g, :, :],
+                        in_=x_raw[g][:].rearrange("p b t (h w) -> p w h b t", w=W)[:, W - 2 : W],
+                    )
+                quantise_x(X_EDGE, 2 * EDGE_COLS)
+            else:
+                lo = ct["x_base"]
+                nc.vector.tensor_copy(
+                    out=x_grouped[:, lo : lo + X_HALF, :].rearrange("p (w h b) t -> p w h b t", w=W, h=H),
+                    in_=x_raw[ct["half"]][:].rearrange("p b t (h w) -> p w h b t", w=W),
+                )
+                quantise_x(lo, MAIN_COLS)
+                quantise_x(lo + MAIN_COLS, STRIP)
 
         w9_codes = keep.tile([P, NP, CO], U32, name="w9_codes", align_bytes=64)
         w9_scales = keep.tile([P, NP, CO], U8, name="w9_scales", align_bytes=64)
         wf_codes = keep.tile([P, NP, C], U32, name="wf_codes", align_bytes=64)
         wf_scales = keep.tile([P, NP, C], U8, name="wf_scales", align_bytes=64)
-        banks_emptied = [0]
 
-        def transpose_and_quantise(raw, codes, scales):
+        def prepare_weight(raw, codes, scales, vector_helps):
             words = raw[:].bitcast(F32)
             grouped = flow.tile([P, PACK * P * PACK], BF16, tag="w_grouped", name="w_grouped", bufs=4, align_bytes=64)
             grouped_words = grouped[:].bitcast(F32)
-            for pair_of_tiles in range(PACK // 2):
+            for j in range(PACK // 2):
                 bank = work.tile([P, PAIR, 2 * P], F32, tag="work", name="w_bank")
                 for i in range(2):
                     for u in range(PAIR):
                         nc.tensor.transpose(
-                            bank[:, u, i * P : (i + 1) * P],
-                            words[:, 2 * pair_of_tiles + i, u * P : (u + 1) * P],
-                            ident[:],
+                            bank[:, u, i * P : (i + 1) * P], words[:, 2 * j + i, u * P : (u + 1) * P], ident[:]
                         )
-                dst = grouped_words[:, pair_of_tiles * 4 * P : (pair_of_tiles + 1) * 4 * P].rearrange(
-                    "p (c u) -> p c u", u=PAIR
-                )
+                dst = grouped_words[:, j * 4 * P : (j + 1) * 4 * P].rearrange("p (c u) -> p c u", u=PAIR)
                 src = bank[:].rearrange("p u c -> p c u")
-                if banks_emptied[0] % 4 == 3:
+                if vector_helps and j == 1:
                     nc.vector.tensor_copy(out=dst, in_=src)
                 else:
                     nc.scalar.copy(out=dst, in_=src)
-                banks_emptied[0] += 1
             nc.vector.quantize_mx(out=codes.bitcast(FP8X4), scales=scales, in_=grouped[:])
-
-        def prepare_weights(k):
-            transpose_and_quantise(w9_raw[k], w9_codes[:, k, :], w9_scales[:, k, :])
-            transpose_and_quantise(wf_raw[k], wf_codes[:, k, :], wf_scales[:, k, :])
 
         planes_of = {}
         cat_of = {}
@@ -236,8 +222,7 @@ def tile_shiftedpillarsconcatentation_bnact_np9_pa_kernel(tc, xa, W9, b9, Wf, b_
             dst_lo = first_row * ct["row"]
             src_lo = (first_row + dh) * ct["row"]
             span = rows * ct["row"]
-            planes = flow.tile([P, PACK, cols], BF16, tag="planes", name="planes")
-            planes_of[n] = planes
+            planes_of[n] = flow.tile([P, PACK, cols], BF16, tag="planes", name="planes")
             for t in range(PACK):
                 y_ps = work.tile([P, cols], F32, tag="work", name="y_ps")
                 nc.tensor.matmul_mx(
@@ -250,7 +235,7 @@ def tile_shiftedpillarsconcatentation_bnact_np9_pa_kernel(tc, xa, W9, b9, Wf, b_
                     stop=True,
                 )
                 nc.scalar.activation(
-                    out=planes[:, t, :].rearrange("p (w s) -> p w s", w=ct["strips"])[
+                    out=planes_of[n][:, t, :].rearrange("p (w s) -> p w s", w=ct["strips"])[
                         :, first_strip:, dst_lo : dst_lo + span
                     ],
                     in_=y_ps[:].rearrange("p (w s) -> p w s", w=ct["strips"])[:, first_strip:, src_lo : src_lo + span],
@@ -259,23 +244,29 @@ def tile_shiftedpillarsconcatentation_bnact_np9_pa_kernel(tc, xa, W9, b9, Wf, b_
                     scale=1.0,
                 )
 
-        def pack(n):
+        def interleave(n):
             ct, k = items[n]
-            cols = ct["strips"] * ct["strip_cols"]
             first_strip, first_row, rows = valid_part(ct, k)
             lo = first_row * ct["row"] // RUN
             hi = lo + rows * ct["row"] // RUN
-            st = stage[(ct["strip_cols"], k)]
             nc.vector.tensor_copy(
-                out=st[:].rearrange("p (w c i) t -> p w c t i", w=ct["strips"], i=RUN)[:, first_strip:, lo:hi],
+                out=stage[(ct["strip_cols"], k)][:].rearrange("p (w c i) t -> p w c t i", w=ct["strips"], i=RUN)[
+                    :, first_strip:, lo:hi
+                ],
                 in_=planes_of[n][:].rearrange("p t (w c i) -> p w c t i", w=ct["strips"], i=RUN)[
                     :, first_strip:, lo:hi
                 ],
             )
+
+        def quantise_cat(n):
+            ct, k = items[n]
+            cols = ct["strips"] * ct["strip_cols"]
             codes = flow.tile([P, cols], U32, tag="cat_codes", name="cat_codes", align_bytes=64)
             scales = flow.tile([P, cols], U8, tag="cat_scales", name="cat_scales", align_bytes=64)
             nc.vector.quantize_mx(
-                out=codes[:].bitcast(FP8X4), scales=scales[:], in_=st[:].rearrange("p c t -> p (c t)")
+                out=codes[:].bitcast(FP8X4),
+                scales=scales[:],
+                in_=stage[(ct["strip_cols"], k)][:].rearrange("p c t -> p (c t)"),
             )
             cat_of[n] = (codes, scales)
 
@@ -316,7 +307,7 @@ def tile_shiftedpillarsconcatentation_bnact_np9_pa_kernel(tc, xa, W9, b9, Wf, b_
                 g = ct["half"]
                 dst = image[:, g * HALF_B : (g + 1) * HALF_B, :, 0 : W - 1]
                 src = acc_of[t][:].rearrange("p (w h b) -> p b h w", w=W - 1, h=H)
-            b_col = bias[:, fuse_bias + t : fuse_bias + t + 1]
+            b_col = bias[:, NP * PACK + t : NP * PACK + t + 1]
             if e == 0:
                 nc.vector.tensor_scalar(out=dst, in0=src, scalar1=b_col, scalar2=None, op0=ADD)
             else:
@@ -331,14 +322,25 @@ def tile_shiftedpillarsconcatentation_bnact_np9_pa_kernel(tc, xa, W9, b9, Wf, b_
                     in_=out_sb[u][:, g * HALF_B : (g + 1) * HALF_B].rearrange("p b e s -> p b (e s)"),
                 )
 
-        for k in range(PREP_AHEAD):
-            prepare_weights(k)
-        for step in range(len(items) + FUSE_LAG):
-            if step + PREP_AHEAD < NP:
-                prepare_weights(step + PREP_AHEAD)
-            if step < len(items):
+        bias_pairs = keep.tile([P, n_rows], F32, name="bias_pairs")
+        bias = keep.tile([P, PAIR * n_rows], F32, name="bias")
+        nc.vector.tensor_copy(out=bias_pairs[:], in_=bias_ps[:, 0:n_rows])
+        nc.vector.tensor_copy(out=bias[:], in_=bias_pairs[:].bitcast(BF16))
+        for step in range(-AHEAD, len(items) + FUSE_LAG):
+            ahead = step + AHEAD
+            packed = step - PACK_LAG
+            fused = step - FUSE_LAG
+            if ahead < len(items) and items[ahead][1] == items[ahead][0]["pillars"][0]:
+                prepare_x(items[ahead][0])
+            if 0 <= packed < len(items):
+                interleave(packed)
+            if ahead < NP:
+                prepare_weight(w9_raw[ahead], w9_codes[:, ahead, :], w9_scales[:, ahead, :], False)
+            if 0 <= packed < len(items):
+                quantise_cat(packed)
+            if ahead < NP:
+                prepare_weight(wf_raw[ahead], wf_codes[:, ahead, :], wf_scales[:, ahead, :], True)
+            if 0 <= step < len(items):
                 project(step)
-            if 0 <= step - PACK_LAG < len(items):
-                pack(step - PACK_LAG)
-            if 0 <= step - FUSE_LAG:
-                fuse(step - FUSE_LAG)
+            if 0 <= fused:
+                fuse(fused)

@@ -76,7 +76,6 @@ def tile_shiftedpillarsconcatentation_bnact_np9_pa_kernel(tc, xa, W9, b9, Wf, b_
     items = [(ct, k) for ct in tiles for k in ct["pillars"]]
 
     with ExitStack() as stack:
-        stack.enter_context(tc.manual_schedule())
         keep = stack.enter_context(tc.tile_pool(name="keep", bufs=1))
         raw_pool = stack.enter_context(tc.tile_pool(name="raw", bufs=RAW_BUFS))
         flow = stack.enter_context(tc.tile_pool(name="flow", bufs=3))
@@ -113,24 +112,25 @@ def tile_shiftedpillarsconcatentation_bnact_np9_pa_kernel(tc, xa, W9, b9, Wf, b_
                     ),
                 )
 
-        load_w9(0)
-        load_x(0)
-        load_wf(0)
-        for k in range(1, NP):
-            load_w9(k)
-            load_wf(k)
-            if k == RAW_BUFS - 1:
-                load_x(1)
-
-        ident = keep.tile([P, P], F32, name="ident")
-        make_identity(nc, ident[:])
-
         bias_rows = keep.tile([P, PAIR * P], BF16, name="bias_rows")
         nc.vector.memset(bias_rows[:], 0.0)
         n_b9 = NP * PAIR
         n_rows = n_b9 + PAIR
-        nc.scalar.dma_start(out=bias_rows[0:n_b9, :], in_=b9.rearrange("k (u c) -> (k u) c", u=PAIR))
-        nc.scalar.dma_start(out=bias_rows[n_b9:n_rows, :], in_=b_fuse.rearrange("(u c) -> u c", u=PAIR))
+        nc.sync.dma_start(out=bias_rows[0:n_b9, :], in_=b9.rearrange("k (u c) -> (k u) c", u=PAIR))
+        nc.sync.dma_start(out=bias_rows[n_b9:n_rows, :], in_=b_fuse.rearrange("(u c) -> u c", u=PAIR))
+        for k in range(NP + FUSE_LAG):
+            if k < NP:
+                load_w9(k)
+            if k == 0:
+                load_x(0)
+            if k == RAW_BUFS - 1:
+                load_x(1)
+            if k >= FUSE_LAG:
+                load_wf(k - FUSE_LAG)
+
+        ident = keep.tile([P, P], F32, name="ident")
+        make_identity(nc, ident[:])
+
         bias_ps = work.tile([P, P], F32, tag="work", name="bias_ps")
         nc.tensor.transpose(bias_ps[:], bias_rows[:].bitcast(F32), ident[:])
 
@@ -338,8 +338,9 @@ def tile_shiftedpillarsconcatentation_bnact_np9_pa_kernel(tc, xa, W9, b9, Wf, b_
                 prepare_weight(w9_raw[ahead], w9_codes[:, ahead, :], w9_scales[:, ahead, :], False)
             if 0 <= packed < len(items):
                 quantise_cat(packed)
-            if ahead < NP:
-                prepare_weight(wf_raw[ahead], wf_codes[:, ahead, :], wf_scales[:, ahead, :], True)
+            if 0 <= ahead - FUSE_LAG < NP:
+                kf = ahead - FUSE_LAG
+                prepare_weight(wf_raw[kf], wf_codes[:, kf, :], wf_scales[:, kf, :], True)
             if 0 <= step < len(items):
                 project(step)
             if 0 <= fused:

@@ -34,7 +34,8 @@ RUN = 4
 RAW_BUFS = 4
 AHEAD = 2
 PACK_LAG = 1
-FUSE_LAG = 2
+FUSE_LAG = 3
+CAT_BUFS = FUSE_LAG - PACK_LAG + 2
 
 
 def column_tiles():
@@ -76,6 +77,7 @@ def tile_shiftedpillarsconcatentation_bnact_np9_pa_kernel(tc, xa, W9, b9, Wf, b_
     items = [(ct, k) for ct in tiles for k in ct["pillars"]]
 
     with ExitStack() as stack:
+        stack.enter_context(tc.manual_schedule())
         keep = stack.enter_context(tc.tile_pool(name="keep", bufs=1))
         raw_pool = stack.enter_context(tc.tile_pool(name="raw", bufs=RAW_BUFS))
         flow = stack.enter_context(tc.tile_pool(name="flow", bufs=3))
@@ -118,15 +120,15 @@ def tile_shiftedpillarsconcatentation_bnact_np9_pa_kernel(tc, xa, W9, b9, Wf, b_
         n_rows = n_b9 + PAIR
         nc.sync.dma_start(out=bias_rows[0:n_b9, :], in_=b9.rearrange("k (u c) -> (k u) c", u=PAIR))
         nc.sync.dma_start(out=bias_rows[n_b9:n_rows, :], in_=b_fuse.rearrange("(u c) -> u c", u=PAIR))
-        for k in range(NP + FUSE_LAG):
+        for k in range(NP + AHEAD):
             if k < NP:
                 load_w9(k)
             if k == 0:
                 load_x(0)
-            if k == RAW_BUFS - 1:
+            if k == NP:
                 load_x(1)
-            if k >= FUSE_LAG:
-                load_wf(k - FUSE_LAG)
+            if k >= AHEAD:
+                load_wf(k - AHEAD)
 
         ident = keep.tile([P, P], F32, name="ident")
         make_identity(nc, ident[:])
@@ -261,8 +263,8 @@ def tile_shiftedpillarsconcatentation_bnact_np9_pa_kernel(tc, xa, W9, b9, Wf, b_
         def quantise_cat(n):
             ct, k = items[n]
             cols = ct["strips"] * ct["strip_cols"]
-            codes = flow.tile([P, cols], U32, tag="cat_codes", name="cat_codes", align_bytes=64)
-            scales = flow.tile([P, cols], U8, tag="cat_scales", name="cat_scales", align_bytes=64)
+            codes = flow.tile([P, cols], U32, tag="cat_codes", name="cat_codes", bufs=CAT_BUFS, align_bytes=64)
+            scales = flow.tile([P, cols], U8, tag="cat_scales", name="cat_scales", bufs=CAT_BUFS, align_bytes=64)
             nc.vector.quantize_mx(
                 out=codes[:].bitcast(FP8X4),
                 scales=scales[:],
@@ -336,12 +338,11 @@ def tile_shiftedpillarsconcatentation_bnact_np9_pa_kernel(tc, xa, W9, b9, Wf, b_
                 interleave(packed)
             if ahead < NP:
                 prepare_weight(w9_raw[ahead], w9_codes[:, ahead, :], w9_scales[:, ahead, :], False)
-            if 0 <= packed < len(items):
-                quantise_cat(packed)
-            if 0 <= ahead - FUSE_LAG < NP:
-                kf = ahead - FUSE_LAG
-                prepare_weight(wf_raw[kf], wf_codes[:, kf, :], wf_scales[:, kf, :], True)
             if 0 <= step < len(items):
                 project(step)
+            if 0 <= packed < len(items):
+                quantise_cat(packed)
+            if 0 <= step < NP:
+                prepare_weight(wf_raw[step], wf_codes[:, step, :], wf_scales[:, step, :], True)
             if 0 <= fused:
                 fuse(fused)

@@ -20,6 +20,7 @@ FLOPS = 2 * NP * CO * C * B * H * W + 2 * C * CO * B * USED
 P = 128
 PACK = 4
 PAIR = 2
+BANK = 512
 HALVES = 2
 HALF_B = B // HALVES
 STRIP = H * HALF_B
@@ -34,8 +35,7 @@ RUN = 4
 RAW_BUFS = 4
 AHEAD = 2
 PACK_LAG = 1
-FUSE_LAG = 3
-CAT_BUFS = FUSE_LAG - PACK_LAG + 2
+FUSE_LAG = 2
 
 
 def column_tiles():
@@ -77,7 +77,6 @@ def tile_shiftedpillarsconcatentation_bnact_np9_pa_kernel(tc, xa, W9, b9, Wf, b_
     items = [(ct, k) for ct in tiles for k in ct["pillars"]]
 
     with ExitStack() as stack:
-        stack.enter_context(tc.manual_schedule())
         keep = stack.enter_context(tc.tile_pool(name="keep", bufs=1))
         raw_pool = stack.enter_context(tc.tile_pool(name="raw", bufs=RAW_BUFS))
         flow = stack.enter_context(tc.tile_pool(name="flow", bufs=3))
@@ -120,15 +119,15 @@ def tile_shiftedpillarsconcatentation_bnact_np9_pa_kernel(tc, xa, W9, b9, Wf, b_
         n_rows = n_b9 + PAIR
         nc.sync.dma_start(out=bias_rows[0:n_b9, :], in_=b9.rearrange("k (u c) -> (k u) c", u=PAIR))
         nc.sync.dma_start(out=bias_rows[n_b9:n_rows, :], in_=b_fuse.rearrange("(u c) -> u c", u=PAIR))
-        for k in range(NP + AHEAD):
+        for k in range(NP + FUSE_LAG):
             if k < NP:
                 load_w9(k)
             if k == 0:
                 load_x(0)
-            if k == NP:
+            if k == RAW_BUFS - 1:
                 load_x(1)
-            if k >= AHEAD:
-                load_wf(k - AHEAD)
+            if k >= FUSE_LAG:
+                load_wf(k - FUSE_LAG)
 
         ident = keep.tile([P, P], F32, name="ident")
         make_identity(nc, ident[:])
@@ -190,7 +189,7 @@ def tile_shiftedpillarsconcatentation_bnact_np9_pa_kernel(tc, xa, W9, b9, Wf, b_
         wf_codes = keep.tile([P, NP, C], U32, name="wf_codes", align_bytes=64)
         wf_scales = keep.tile([P, NP, C], U8, name="wf_scales", align_bytes=64)
 
-        def prepare_weight(raw, codes, scales, vector_helps):
+        def prepare_weight(raw, codes, scales):
             words = raw[:].bitcast(F32)
             grouped = flow.tile([P, PACK * P * PACK], BF16, tag="w_grouped", name="w_grouped", bufs=4, align_bytes=64)
             grouped_words = grouped[:].bitcast(F32)
@@ -203,10 +202,10 @@ def tile_shiftedpillarsconcatentation_bnact_np9_pa_kernel(tc, xa, W9, b9, Wf, b_
                         )
                 dst = grouped_words[:, j * 4 * P : (j + 1) * 4 * P].rearrange("p (c u) -> p c u", u=PAIR)
                 src = bank[:].rearrange("p u c -> p c u")
-                if vector_helps and j == 1:
-                    nc.vector.tensor_copy(out=dst, in_=src)
-                else:
+                if j == 0:
                     nc.scalar.copy(out=dst, in_=src)
+                else:
+                    nc.vector.tensor_copy(out=dst, in_=src)
             nc.vector.quantize_mx(out=codes.bitcast(FP8X4), scales=scales, in_=grouped[:])
 
         planes_of = {}
@@ -224,11 +223,10 @@ def tile_shiftedpillarsconcatentation_bnact_np9_pa_kernel(tc, xa, W9, b9, Wf, b_
             dst_lo = first_row * ct["row"]
             src_lo = (first_row + dh) * ct["row"]
             span = rows * ct["row"]
-            planes_of[n] = flow.tile([P, PACK, cols], BF16, tag="planes", name="planes")
-            for t in range(PACK):
-                y_ps = work.tile([P, cols], F32, tag="work", name="y_ps")
+
+            def project_row_tile(t, y_ps):
                 nc.tensor.matmul_mx(
-                    out=y_ps[:],
+                    out=y_ps,
                     lhsT=w9_codes[:, k, t * P : (t + 1) * P].bitcast(FP8X4),
                     lhsT_scale=w9_scales[:, k, t * P : (t + 1) * P],
                     rhs=x_codes[:, x_lo : x_lo + cols].bitcast(FP8X4),
@@ -236,6 +234,22 @@ def tile_shiftedpillarsconcatentation_bnact_np9_pa_kernel(tc, xa, W9, b9, Wf, b_
                     start=True,
                     stop=True,
                 )
+
+            if PACK * cols <= BANK:
+                y_bank = work.tile([P, PACK, cols], F32, tag="work", name="y_bank")
+                for t in range(PACK):
+                    project_row_tile(t, y_bank[:, t, :])
+                nc.vector.tensor_tensor(
+                    out=stage[(ct["strip_cols"], k)][:, dst_lo : dst_lo + span, :],
+                    in0=y_bank[:, :, src_lo : src_lo + span].rearrange("p t c -> p c t"),
+                    in1=bias[:, k * PACK : (k + 1) * PACK].unsqueeze(1).to_broadcast([P, span, PACK]),
+                    op=ADD,
+                )
+                return
+            planes_of[n] = flow.tile([P, PACK, cols], BF16, tag="planes", name="planes")
+            for t in range(PACK):
+                y_ps = work.tile([P, cols], F32, tag="work", name="y_ps")
+                project_row_tile(t, y_ps[:])
                 nc.scalar.activation(
                     out=planes_of[n][:, t, :].rearrange("p (w s) -> p w s", w=ct["strips"])[
                         :, first_strip:, dst_lo : dst_lo + span
@@ -247,6 +261,8 @@ def tile_shiftedpillarsconcatentation_bnact_np9_pa_kernel(tc, xa, W9, b9, Wf, b_
                 )
 
         def interleave(n):
+            if n not in planes_of:
+                return
             ct, k = items[n]
             first_strip, first_row, rows = valid_part(ct, k)
             lo = first_row * ct["row"] // RUN
@@ -263,8 +279,8 @@ def tile_shiftedpillarsconcatentation_bnact_np9_pa_kernel(tc, xa, W9, b9, Wf, b_
         def quantise_cat(n):
             ct, k = items[n]
             cols = ct["strips"] * ct["strip_cols"]
-            codes = flow.tile([P, cols], U32, tag="cat_codes", name="cat_codes", bufs=CAT_BUFS, align_bytes=64)
-            scales = flow.tile([P, cols], U8, tag="cat_scales", name="cat_scales", bufs=CAT_BUFS, align_bytes=64)
+            codes = flow.tile([P, cols], U32, tag="cat_codes", name="cat_codes", align_bytes=64)
+            scales = flow.tile([P, cols], U8, tag="cat_scales", name="cat_scales", align_bytes=64)
             nc.vector.quantize_mx(
                 out=codes[:].bitcast(FP8X4),
                 scales=scales[:],
@@ -337,12 +353,13 @@ def tile_shiftedpillarsconcatentation_bnact_np9_pa_kernel(tc, xa, W9, b9, Wf, b_
             if 0 <= packed < len(items):
                 interleave(packed)
             if ahead < NP:
-                prepare_weight(w9_raw[ahead], w9_codes[:, ahead, :], w9_scales[:, ahead, :], False)
-            if 0 <= step < len(items):
-                project(step)
+                prepare_weight(w9_raw[ahead], w9_codes[:, ahead, :], w9_scales[:, ahead, :])
             if 0 <= packed < len(items):
                 quantise_cat(packed)
-            if 0 <= step < NP:
-                prepare_weight(wf_raw[step], wf_codes[:, step, :], wf_scales[:, step, :], True)
+            if 0 <= ahead - FUSE_LAG < NP:
+                kf = ahead - FUSE_LAG
+                prepare_weight(wf_raw[kf], wf_codes[:, kf, :], wf_scales[:, kf, :])
+            if 0 <= step < len(items):
+                project(step)
             if 0 <= fused:
                 fuse(fused)

from contextlib import ExitStack

import concourse.mybir as mybir
from concourse.masks import make_identity

F32 = mybir.dt.float32
BF16 = mybir.dt.bfloat16
I32 = mybir.dt.int32
U32 = mybir.dt.uint32
U8 = mybir.dt.uint8
FP8X4 = mybir.dt.float8_e4m3fn_x4
IDENTITY = mybir.ActivationFunctionType.Identity
ADD = mybir.AluOpType.add

B, C, H, W, NP, CO = 16, 512, 8, 9, 9, 512
SHIFTS = ((0, 0), (0, 0), (0, 0), (0, -1), (0, 1), (1, -1), (1, 1), (-1, -1), (-1, 1))
USED = sum((H - abs(dh)) * (W - abs(dw)) for dh, dw in SHIFTS)
FLOPS = 2 * NP * CO * C * B * H * W + 2 * C * CO * B * USED

P = 128
PACK = 4
PAIR = 2
BANK = 512
HALVES = 2
HALF_B = B // HALVES
STRIP = H * HALF_B
MAIN_COLS = (W - 1) * STRIP
EDGE_COLS = H * B
X_HALF = W * STRIP
X_PAD = STRIP
X_EDGE = X_PAD + HALVES * X_HALF
X_COLS = X_EDGE + 2 * EDGE_COLS
RUN = 4

RAW_BUFS = 4
AHEAD = 2
PACK_LAG = 1
FUSE_LAG = 2


def column_tiles():
    main = [
        dict(
            name="main%d" % g,
            half=g,
            strips=W - 1,
            strip_cols=STRIP,
            row=HALF_B,
            x_base=X_PAD + g * X_HALF,
            x_step=STRIP,
            pillars=list(range(NP)),
        )
        for g in range(HALVES)
    ]
    edge = dict(
        name="edge",
        half=None,
        strips=1,
        strip_cols=EDGE_COLS,
        row=B,
        x_base=X_EDGE + EDGE_COLS,
        x_step=EDGE_COLS,
        pillars=[k for k in range(NP) if SHIFTS[k][1] <= 0],
    )
    return [main[0], edge, main[1]]


def valid_part(ct, k):
    dh, dw = SHIFTS[k]
    first_strip = 1 if (ct["half"] is not None and dw < 0) else 0
    return first_strip, max(-dh, 0), H - abs(dh)


def tile_shiftedpillarsconcatentation_bnact_np9_pa_kernel(tc, xa, W9, b9, Wf, b_fuse, out):
    nc = tc.nc
    tiles = column_tiles()
    items = [(ct, k) for ct in tiles for k in ct["pillars"]]

    with ExitStack() as stack:
        keep = stack.enter_context(tc.tile_pool(name="keep", bufs=1))
        raw_pool = stack.enter_context(tc.tile_pool(name="raw", bufs=RAW_BUFS))
        flow = stack.enter_context(tc.tile_pool(name="flow", bufs=3))
        work = stack.enter_context(tc.psum_pool(name="work", bufs=4))
        accs = stack.enter_context(tc.psum_pool(name="accs", bufs=PACK))

        x_raw = {}
        w9_raw = {}
        wf_raw = {}

        def load_x(g):
            x_raw[g] = keep.tile([P, HALF_B, PACK, H * W], BF16, name="x_raw%d" % g)
            nc.sync.dma_start(
                out=x_raw[g][:].rearrange("p b (u e) s -> p (b u) (e s)", u=PAIR),
                in_=xa[g * HALF_B : (g + 1) * HALF_B].rearrange(
                    "b (u p e) h w -> p (b u) (e h w)", u=PAIR, e=PAIR
                ),
            )

        def load_w9(k):
            w9_raw[k] = raw_pool.tile([P, PACK, C], BF16, tag="w9_raw", name="w9_raw%d" % k)
            nc.sync.dma_start(
                out=w9_raw[k][:].rearrange("p (u e) c -> p u (e c)", u=PAIR),
                in_=W9[k].rearrange("(u p e) c -> p u (e c)", u=PAIR, e=PAIR),
            )

        def load_wf(k):
            wf_raw[k] = raw_pool.tile([P, PACK, CO], BF16, tag="wf_raw", name="wf_raw%d" % k)
            for u in range(PAIR):
                nc.sync.dma_start(
                    out=wf_raw[k][:, PAIR * u : PAIR * (u + 1), :],
                    in_=Wf[u * PAIR * P : (u + 1) * PAIR * P, k * CO : (k + 1) * CO].rearrange(
                        "(p e) j -> p e j", e=PAIR
                    ),
                )

        bias_rows = keep.tile([P, PAIR * P], BF16, name="bias_rows")
        nc.vector.memset(bias_rows[:], 0.0)
        n_b9 = NP * PAIR
        n_rows = n_b9 + PAIR
        nc.sync.dma_start(out=bias_rows[0:n_b9, :], in_=b9.rearrange("k (u c) -> (k u) c", u=PAIR))
        nc.sync.dma_start(out=bias_rows[n_b9:n_rows, :], in_=b_fuse.rearrange("(u c) -> u c", u=PAIR))
        for k in range(NP + FUSE_LAG):
            if k < NP:
                load_w9(k)
            if k == 0:
                load_x(0)
            if k == RAW_BUFS - 1:
                load_x(1)
            if k >= FUSE_LAG:
                load_wf(k - FUSE_LAG)

        ident = keep.tile([P, P], F32, name="ident")
        make_identity(nc, ident[:])

        bias_ps = work.tile([P, P], F32, tag="work", name="bias_ps")
        nc.tensor.transpose(bias_ps[:], bias_rows[:].bitcast(F32), ident[:])

        stage = {}
        for ct in tiles:
            for k in ct["pillars"]:
                key = (ct["strip_cols"], k)
                if key in stage:
                    continue
                stage[key] = keep.tile(
                    [P, ct["strips"] * ct["strip_cols"], PACK], BF16, name="stage%d_%d" % key, align_bytes=64
                )
                first_strip, first_row, rows = valid_part(ct, k)
                view = stage[key][:].rearrange("p (w s) t -> p w s t", w=ct["strips"])
                if first_strip:
                    nc.vector.memset(view[:, 0:first_strip], 0.0)
                if rows < H:
                    empty_row = 0 if first_row else H - 1
                    nc.vector.memset(view[:, :, empty_row * ct["row"] : (empty_row + 1) * ct["row"], :], 0.0)

        x_grouped = keep.tile([P, X_COLS, PACK], BF16, name="x_grouped", align_bytes=64)
        x_codes = keep.tile([P, X_COLS], U32, name="x_codes", align_bytes=64)
        x_scales = keep.tile([P, X_COLS], U8, name="x_scales", align_bytes=64)
        nc.vector.memset(x_codes[:, 0:X_PAD].bitcast(I32), 0)
        nc.vector.memset(x_scales[:, 0:X_PAD].bitcast(I32), 0)

        def quantise_x(lo, cols):
            nc.vector.quantize_mx(
                out=x_codes[:, lo : lo + cols].bitcast(FP8X4),
                scales=x_scales[:, lo : lo + cols],
                in_=x_grouped[:, lo : lo + cols, :].rearrange("p c t -> p (c t)"),
            )

        def prepare_x(ct):
            if ct["half"] is None:
                for g in range(HALVES):
                    nc.vector.tensor_copy(
                        out=x_grouped[:, X_EDGE:X_COLS, :].rearrange(
                            "p (w h g b) t -> p w h g b t", w=2, h=H, g=HALVES
                        )[:, :, :, g, :, :],
                        in_=x_raw[g][:].rearrange("p b t (h w) -> p w h b t", w=W)[:, W - 2 : W],
                    )
                quantise_x(X_EDGE, 2 * EDGE_COLS)
            else:
                lo = ct["x_base"]
                nc.vector.tensor_copy(
                    out=x_grouped[:, lo : lo + X_HALF, :].rearrange("p (w h b) t -> p w h b t", w=W, h=H),
                    in_=x_raw[ct["half"]][:].rearrange("p b t (h w) -> p w h b t", w=W),
                )
                quantise_x(lo, MAIN_COLS)
                quantise_x(lo + MAIN_COLS, STRIP)

        w9_codes = keep.tile([P, NP, CO], U32, name="w9_codes", align_bytes=64)
        w9_scales = keep.tile([P, NP, CO], U8, name="w9_scales", align_bytes=64)
        wf_codes = keep.tile([P, NP, C], U32, name="wf_codes", align_bytes=64)
        wf_scales = keep.tile([P, NP, C], U8, name="wf_scales", align_bytes=64)

        def prepare_weight(raw, codes, scales):
            words = raw[:].bitcast(F32)
            grouped = flow.tile([P, PACK * P * PACK], BF16, tag="w_grouped", name="w_grouped", bufs=4, align_bytes=64)
            grouped_words = grouped[:].bitcast(F32)
            for j in range(PACK // 2):
                bank = work.tile([P, PAIR, 2 * P], F32, tag="work", name="w_bank")
                for i in range(2):
                    for u in range(PAIR):
                        nc.tensor.transpose(
                            bank[:, u, i * P : (i + 1) * P], words[:, 2 * j + i, u * P : (u + 1) * P], ident[:]
                        )
                dst = grouped_words[:, j * 4 * P : (j + 1) * 4 * P].rearrange("p (c u) -> p c u", u=PAIR)
                src = bank[:].rearrange("p u c -> p c u")
                if j == 0:
                    nc.scalar.copy(out=dst, in_=src)
                else:
                    nc.vector.tensor_copy(out=dst, in_=src)
            nc.vector.quantize_mx(out=codes.bitcast(FP8X4), scales=scales, in_=grouped[:])

        planes_of = {}
        cat_of = {}
        acc_of = {}
        out_sb = [keep.tile([P, B, PAIR, H * W], F32, name="out_sb%d" % u) for u in range(PAIR)]
        finished = set()

        def project(n):
            ct, k = items[n]
            dh, dw = SHIFTS[k]
            cols = ct["strips"] * ct["strip_cols"]
            x_lo = ct["x_base"] + dw * ct["x_step"]
            first_strip, first_row, rows = valid_part(ct, k)
            dst_lo = first_row * ct["row"]
            src_lo = (first_row + dh) * ct["row"]
            span = rows * ct["row"]

            def project_row_tile(t, y_ps):
                nc.tensor.matmul_mx(
                    out=y_ps,
                    lhsT=w9_codes[:, k, t * P : (t + 1) * P].bitcast(FP8X4),
                    lhsT_scale=w9_scales[:, k, t * P : (t + 1) * P],
                    rhs=x_codes[:, x_lo : x_lo + cols].bitcast(FP8X4),
                    rhs_scale=x_scales[:, x_lo : x_lo + cols],
                    start=True,
                    stop=True,
                )

            if PACK * cols <= BANK:
                y_bank = work.tile([P, PACK, cols], F32, tag="work", name="y_bank")
                for t in range(PACK):
                    project_row_tile(t, y_bank[:, t, :])
                nc.vector.tensor_tensor(
                    out=stage[(ct["strip_cols"], k)][:, dst_lo : dst_lo + span, :],
                    in0=y_bank[:, :, src_lo : src_lo + span].rearrange("p t c -> p c t"),
                    in1=bias[:, k * PACK : (k + 1) * PACK].unsqueeze(1).to_broadcast([P, span, PACK]),
                    op=ADD,
                )
                return
            planes_of[n] = flow.tile([P, PACK, cols], BF16, tag="planes", name="planes")
            for t in range(PACK):
                y_ps = work.tile([P, cols], F32, tag="work", name="y_ps")
                project_row_tile(t, y_ps[:])
                nc.scalar.activation(
                    out=planes_of[n][:, t, :].rearrange("p (w s) -> p w s", w=ct["strips"])[
                        :, first_strip:, dst_lo : dst_lo + span
                    ],
                    in_=y_ps[:].rearrange("p (w s) -> p w s", w=ct["strips"])[:, first_strip:, src_lo : src_lo + span],
                    func=IDENTITY,
                    bias=bias[:, k * PACK + t : k * PACK + t + 1],
                    scale=1.0,
                )

        def interleave(n):
            if n not in planes_of:
                return
            ct, k = items[n]
            first_strip, first_row, rows = valid_part(ct, k)
            lo = first_row * ct["row"] // RUN
            hi = lo + rows * ct["row"] // RUN
            nc.vector.tensor_copy(
                out=stage[(ct["strip_cols"], k)][:].rearrange("p (w c i) t -> p w c t i", w=ct["strips"], i=RUN)[
                    :, first_strip:, lo:hi
                ],
                in_=planes_of[n][:].rearrange("p t (w c i) -> p w c t i", w=ct["strips"], i=RUN)[
                    :, first_strip:, lo:hi
                ],
            )

        def quantise_cat(n):
            ct, k = items[n]
            cols = ct["strips"] * ct["strip_cols"]
            codes = flow.tile([P, cols], U32, tag="cat_codes", name="cat_codes", align_bytes=64)
            scales = flow.tile([P, cols], U8, tag="cat_scales", name="cat_scales", align_bytes=64)
            nc.vector.quantize_mx(
                out=codes[:].bitcast(FP8X4),
                scales=scales[:],
                in_=stage[(ct["strip_cols"], k)][:].rearrange("p c t -> p (c t)"),
            )
            cat_of[n] = (codes, scales)

        def fuse(n):
            ct, k = items[n]
            cols = ct["strips"] * ct["strip_cols"]
            codes, scales = cat_of[n]
            first = k == ct["pillars"][0]
            last = k == ct["pillars"][-1]
            for t in range(PACK):
                if first:
                    acc_of[t] = accs.tile([P, cols], F32, tag="acc", name="acc")
                nc.tensor.matmul_mx(
                    out=acc_of[t][:],
                    lhsT=wf_codes[:, k, t * P : (t + 1) * P].bitcast(FP8X4),
                    lhsT_scale=wf_scales[:, k, t * P : (t + 1) * P],
                    rhs=codes[:].bitcast(FP8X4),
                    rhs_scale=scales[:],
                    start=first,
                    stop=last,
                )
            if last:
                for t in range(PACK):
                    empty_accumulator(ct, t)
                finished.add(ct["name"])
                for g in range(HALVES):
                    if ("main%d" % g) in finished and "edge" in finished and ("stored%d" % g) not in finished:
                        finished.add("stored%d" % g)
                        store(g)

        def empty_accumulator(ct, t):
            u, e = divmod(t, PAIR)
            image = out_sb[u][:, :, e, :].rearrange("p b (h w) -> p b h w", w=W)
            if ct["half"] is None:
                dst = image[:, :, :, W - 1]
                src = acc_of[t][:].rearrange("p (h b) -> p b h", h=H)
            else:
                g = ct["half"]
                dst = image[:, g * HALF_B : (g + 1) * HALF_B, :, 0 : W - 1]
                src = acc_of[t][:].rearrange("p (w h b) -> p b h w", w=W - 1, h=H)
            b_col = bias[:, NP * PACK + t : NP * PACK + t + 1]
            if e == 0:
                nc.vector.tensor_scalar(out=dst, in0=src, scalar1=b_col, scalar2=None, op0=ADD)
            else:
                nc.scalar.activation(out=dst, in_=src, func=IDENTITY, bias=b_col, scale=1.0)

        def store(g):
            for u in range(PAIR):
                nc.sync.dma_start(
                    out=out[g * HALF_B : (g + 1) * HALF_B, u * PAIR * P : (u + 1) * PAIR * P].rearrange(
                        "b (p e) h w -> p b (e h w)", e=PAIR
                    ),
                    in_=out_sb[u][:, g * HALF_B : (g + 1) * HALF_B].rearrange("p b e s -> p b (e s)"),
                )

        bias_pairs = keep.tile([P, n_rows], F32, name="bias_pairs")
        bias = keep.tile([P, PAIR * n_rows], F32, name="bias")
        nc.vector.tensor_copy(out=bias_pairs[:], in_=bias_ps[:, 0:n_rows])
        nc.vector.tensor_copy(out=bias[:], in_=bias_pairs[:].bitcast(BF16))
        for step in range(-AHEAD, len(items) + FUSE_LAG):
            ahead = step + AHEAD
            packed = step - PACK_LAG
            fused = step - FUSE_LAG
            if ahead < len(items) and items[ahead][1] == items[ahead][0]["pillars"][0]:
                prepare_x(items[ahead][0])
            if 0 <= packed < len(items):
                interleave(packed)
            if ahead < NP:
                prepare_weight(w9_raw[ahead], w9_codes[:, ahead, :], w9_scales[:, ahead, :])
            if 0 <= packed < len(items):
                quantise_cat(packed)
            if 0 <= ahead - FUSE_LAG < NP:
                kf = ahead - FUSE_LAG
                prepare_weight(wf_raw[kf], wf_codes[:, kf, :], wf_scales[:, kf, :])
            if 0 <= step < len(items):
                project(step)
            if 0 <= fused:
                fuse(fused)
